import numpy as np
import ml_dtypes


def mxq(x, axis, fmt="e4m3"):
    dtype, down = {"e4m3": (ml_dtypes.float8_e4m3fn, 7), "e5m2": (ml_dtypes.float8_e5m2, 14)}[fmt]
    v = np.moveaxis(np.asarray(x, np.float32).astype(ml_dtypes.bfloat16).astype(np.float64), axis, -1)
    blocks = v.reshape(v.shape[:-1] + (-1, 32))
    amax = np.abs(blocks).max(-1, keepdims=True)
    byte = np.maximum(np.where(amax > 0, np.frexp(amax)[1] - 1 + 127, 0) - down, 1)
    scale = np.exp2(byte - 127.0)
    codes = (blocks / scale).astype(np.float32).astype(dtype).astype(np.float64)
    return np.moveaxis((codes * scale).reshape(v.shape), -1, axis)


WIDE = False


def mx_kscale(k):
    if not WIDE:
        return np.ones(k)
    levels = np.array([10, -10, 5, -5, 0])
    if k % 512:
        return np.exp2(np.random.permutation(np.resize(levels, k // 32))).repeat(32)
    a = np.empty((k // 512, 16))
    for p in range(k // 512):
        a[p, :8] = np.random.permutation(np.resize(levels, 8))
        for g in range(8):
            far = levels[np.abs(levels - a[p, g]) >= 10]
            a[p, g + 8] = far[np.random.randint(len(far))]
    return np.exp2(a.ravel()).repeat(32)


BF16 = ml_dtypes.bfloat16


def bf(x):
    return np.asarray(x, np.float32).astype(BF16)


def f64(x):
    return np.asarray(x).astype(np.float64)


B, N, E, H, G, C, EO = 1, 2048, 1024, 8, 128, 512, 1024
LN_EPS = 1e-5


def sigmoid(v):
    return 1.0 / (1.0 + np.exp(-v))


def layernorm(y, w, b):
    mu = y.mean(-1, keepdims=True)
    var = np.square(y - mu).mean(-1, keepdims=True)
    return (y - mu) / np.sqrt(var + LN_EPS) * w + b


def setup_inputs():
    s = mx_kscale(E)
    return {"attn": bf((1.5 + 2.5 * np.random.standard_normal((B, N, E))) * s),
            "gate_low": bf(np.random.standard_normal((B, N, G))),
            "Wg2": bf(np.random.standard_normal((G, E)) / np.sqrt(G)),
            "Wo": bf(np.random.standard_normal((E, EO)) / np.sqrt(E) / s[:, None]),
            "ln_w": bf(1.0 + 0.1 * np.random.standard_normal(EO)),
            "ln_b": bf(0.1 * np.random.standard_normal(EO))}


def reference(attn, gate_low, Wg2, Wo, ln_w, ln_b):
    gate = sigmoid(f64(gate_low) @ f64(Wg2))
    h = f64(attn) * gate
    y = mxq(h, 2, "e4m3") @ mxq(f64(Wo), 0, "e4m3")
    return layernorm(y, f64(ln_w), f64(ln_b))

@@ -1,0 +1,309 @@
+from contextlib import ExitStack
+
+import concourse.mybir as mybir
+from concourse.masks import make_identity
+
+F32 = mybir.dt.float32
+BF16 = mybir.dt.bfloat16
+U32 = mybir.dt.uint32
+U8 = mybir.dt.uint8
+FP8X4 = mybir.dt.float8_e4m3fn_x4
+ACT = mybir.ActivationFunctionType
+ALU = mybir.AluOpType
+
+P = 128
+TOKENS = 2048
+E = 1024
+D_GATE = 128
+E_OUT = 1024
+LN_EPS = 1e-5
+
+TILES = TOKENS // P
+PAIRS = TILES // 2
+PAIR_TOKENS = 2 * P
+PACK = 4
+PASSES = E // (P * PACK)
+UNITS = PAIRS * PASSES
+BANK = 512
+HALVES = E_OUT // BANK
+WO_CHUNK = 128
+WO_CHUNKS_PER_PASS = E_OUT // WO_CHUNK
+WO_CHUNKS = PASSES * WO_CHUNKS_PER_PASS
+WO_FIRST_UNIT = 2
+
+FLOPS = 2 * TOKENS * E * E_OUT + 2 * TOKENS * D_GATE * E
+
+
+def tile_tnlattention_pb_kernel(tc, attn, gate_low, Wg2, Wo, ln_w, ln_b, out):
+    nc = tc.nc
+    attn_rows = attn.flatten_outer_dims().rearrange("(p i) e -> p (i e)", i=TILES)
+    gate_low_rows = gate_low.flatten_outer_dims().rearrange("(p i) d -> p (i d)", i=TILES)
+    out_rows = out.flatten_outer_dims().rearrange("(p i) n -> p (i n)", i=TILES)
+
+    with ExitStack() as stack:
+        keep = stack.enter_context(tc.tile_pool(name="keep", bufs=1))
+        stage1 = stack.enter_context(tc.tile_pool(name="stage1", bufs=3))
+        stage2 = stack.enter_context(tc.tile_pool(name="stage2", bufs=4))
+        psum_keep = stack.enter_context(tc.psum_pool(name="psum_keep", bufs=1))
+        psum = stack.enter_context(tc.psum_pool(name="psum", bufs=6))
+
+        wg2_sb = keep.tile([P, E], BF16)
+        gate_low_sb = keep.tile([P, TILES * D_GATE], BF16)
+        attn_sb = keep.tile([P, TILES * E], BF16)
+        wo_raw = keep.tile([P, PASSES, PACK, E_OUT], BF16)
+        for pair in range(PAIRS):
+            gate_cols = slice(pair * 2 * D_GATE, (pair + 1) * 2 * D_GATE)
+            nc.sync.dma_start(out=gate_low_sb[:, gate_cols], in_=gate_low_rows[:, gate_cols])
+            if pair == 0:
+                nc.sync.dma_start(out=wg2_sb[:], in_=Wg2)
+            attn_cols = slice(pair * 2 * E, (pair + 1) * 2 * E)
+            nc.sync.dma_start(out=attn_sb[:, attn_cols], in_=attn_rows[:, attn_cols])
+            if 1 <= pair <= PASSES:
+                g = pair - 1
+                nc.sync.dma_start(
+                    out=wo_raw[:, g],
+                    in_=Wo[g * P * PACK : (g + 1) * P * PACK, :].rearrange(
+                        "(p t) n -> p t n", t=PACK
+                    ),
+                )
+        ln_w_rows = keep.tile([P, E_OUT], BF16)
+        nc.sync.dma_start(out=ln_w_rows[:], in_=ln_w.partition_broadcast(P))
+        ln_b_rows = keep.tile([P, E_OUT], BF16)
+        nc.sync.dma_start(out=ln_b_rows[:], in_=ln_b.partition_broadcast(P))
+
+        ident_bf16 = keep.tile([P, P], BF16)
+        make_identity(nc, ident_bf16[:])
+        ident_f32 = keep.tile([P, P], F32)
+        make_identity(nc, ident_f32[:])
+        minus_half = keep.tile([P, 1], F32)
+        nc.gpsimd.memset(minus_half[:], -0.5)
+
+        table_in = keep.tile([P, 1], F32)
+        nc.vector.memset(table_in[:], 0.0)
+        table_out = keep.tile([P, 1], F32)
+        nc.scalar.activation(out=table_out[:], in_=table_in[:], func=ACT.Sigmoid)
+
+        wg2_by_word = wg2_sb[:].rearrange("d (g p t) -> d g t p", g=PASSES, t=PACK)
+        attn_words = attn_sb[:].bitcast(F32)
+
+        wo_grouped = keep.tile([P, PASSES, E_OUT, PACK], BF16, align_bytes=64)
+        wo_codes = keep.tile([P, PASSES, E_OUT], U32, align_bytes=64)
+        wo_scales = keep.tile([P, PASSES, E_OUT], U8, align_bytes=64)
+        h_codes = keep.tile([P, PAIRS, PASSES, PAIR_TOKENS], U32, align_bytes=64)
+        h_scales = keep.tile([P, PAIRS, PASSES, PAIR_TOKENS], U8, align_bytes=64)
+        gate_lowT = keep.tile([P, TILES * P], BF16)
+
+        def wo_chunk(chunk):
+            g, quarter = divmod(chunk, WO_CHUNKS_PER_PASS)
+            return g, slice(quarter * WO_CHUNK, (quarter + 1) * WO_CHUNK)
+
+        def regroup_wo(chunk):
+            g, cols = wo_chunk(chunk)
+            grouped = wo_grouped[:, g, cols, :].rearrange("p (c i) t -> p c t i", i=4)
+            raw = wo_raw[:, g, :, cols].rearrange("p t (c i) -> p c t i", i=4)
+            nc.scalar.copy(out=grouped, in_=raw)
+
+        def quantise_wo(chunk):
+            g, cols = wo_chunk(chunk)
+            nc.vector.quantize_mx(
+                out=wo_codes[:, g, cols].bitcast(FP8X4),
+                scales=wo_scales[:, g, cols],
+                in_=wo_grouped[:, g, cols, :].rearrange("p n t -> p (n t)"),
+            )
+
+        def turn_gate_low(pair):
+            turned = psum.tile([P, PAIR_TOKENS], BF16, tag="bank")
+            for half in range(2):
+                i = 2 * pair + half
+                nc.tensor.transpose(
+                    out=turned[:, half * P : (half + 1) * P],
+                    in_=gate_low_sb[:, i * D_GATE : (i + 1) * D_GATE],
+                    identity=ident_bf16[:],
+                )
+            nc.vector.tensor_copy(
+                out=gate_lowT[:, pair * PAIR_TOKENS : (pair + 1) * PAIR_TOKENS], in_=turned[:]
+            )
+
+        def gated_unit(pair, g, h_grouped):
+            sig = stage1.tile([P, PAIR_TOKENS, PACK], F32)
+            for half in range(2):
+                i = 2 * pair + half
+                gateT = psum.tile([P, PACK, P], F32, tag="bank")
+                for t in range(PACK):
+                    nc.tensor.matmul(
+                        out=gateT[:, t, :],
+                        lhsT=wg2_by_word[:, g, t, :],
+                        rhs=gate_lowT[:, i * P : (i + 1) * P],
+                        start=True,
+                        stop=True,
+                    )
+                nc.scalar.activation(
+                    out=sig[:, half * P : (half + 1) * P, :],
+                    in_=gateT[:].rearrange("p t m -> p m t"),
+                    func=ACT.Sigmoid,
+                )
+            attnT = psum.tile([P, BANK], F32, tag="bank")
+            for u in range(2):
+                for half in range(2):
+                    word0 = (2 * pair + half) * (E // 2) + 2 * g * P + u
+                    nc.tensor.transpose(
+                        out=attnT[:, (2 * u + half) * P : (2 * u + half + 1) * P],
+                        in_=attn_words[:, word0 : word0 + 2 * P - 1 : 2],
+                        identity=ident_f32[:],
+                    )
+            nc.vector.tensor_tensor(
+                out=h_grouped[:, g].rearrange("p m (u e) -> p m u e", e=2),
+                in0=attnT[:].bitcast(BF16).rearrange("p (u m e) -> p m u e", u=2, e=2),
+                in1=sig[:].rearrange("p m (u e) -> p m u e", e=2),
+                op=ALU.mult,
+            )
+
+        def quantise_h(pair, h_grouped):
+            nc.vector.quantize_mx(
+                out=h_codes[:, pair].rearrange("p g m -> p (g m)").bitcast(FP8X4),
+                scales=h_scales[:, pair].rearrange("p g m -> p (g m)"),
+                in_=h_grouped[:].rearrange("p g m t -> p (g m t)"),
+            )
+
+        h_grouped_of = {}
+        turn_gate_low(0)
+        for step in range(UNITS + WO_FIRST_UNIT + 1):
+            pair, g = divmod(step, PASSES)
+            if step < UNITS:
+                if g == 0:
+                    h_grouped = stage1.tile([P, PASSES, PAIR_TOKENS, PACK], BF16, align_bytes=64)
+                    h_grouped_of[pair] = h_grouped
+                if g == PASSES - 1 and pair + 1 < PAIRS:
+                    turn_gate_low(pair + 1)
+                gated_unit(pair, g, h_grouped_of[pair])
+            chunk = step - WO_FIRST_UNIT
+            if 0 <= chunk < WO_CHUNKS:
+                regroup_wo(chunk)
+            if 0 <= chunk - 1 < WO_CHUNKS:
+                quantise_wo(chunk - 1)
+            if g == 0 and 1 <= pair <= PAIRS:
+                quantise_h(pair - 1, h_grouped_of[pair - 1])
+
+        y_of = {}
+        y_copy_of = {}
+        neg_mean_of = {}
+        rstd_of = {}
+        centred_of = {}
+
+        def project(i):
+            pair, half = divmod(i, 2)
+            tokens = slice(half * P, (half + 1) * P)
+            banks = []
+            for n_half in range(HALVES):
+                cols = slice(n_half * BANK, (n_half + 1) * BANK)
+                y = psum.tile([P, BANK], F32, tag="bank")
+                for g in range(PASSES):
+                    nc.tensor.matmul_mx(
+                        out=y[:],
+                        lhsT=h_codes[:, pair, g, tokens].bitcast(FP8X4),
+                        lhsT_scale=h_scales[:, pair, g, tokens],
+                        rhs=wo_codes[:, g, cols].bitcast(FP8X4),
+                        rhs_scale=wo_scales[:, g, cols],
+                        start=(g == 0),
+                        stop=(g == PASSES - 1),
+                    )
+                banks.append(y)
+            y_of[i] = banks
+
+        def row_means(i):
+            y_copy = stage2.tile([P, E_OUT], F32)
+            sums = stage2.tile([P, HALVES], F32)
+            for n_half in range(HALVES):
+                nc.scalar.activation(
+                    out=y_copy[:, n_half * BANK : (n_half + 1) * BANK],
+                    in_=y_of[i][n_half][:],
+                    func=ACT.Identity,
+                    accum_out=sums[:, n_half : n_half + 1],
+                )
+            neg_mean = stage2.tile([P, 1], F32)
+            nc.gpsimd.tensor_scalar(
+                out=neg_mean[:],
+                in0=sums[:, 0:1],
+                scalar1=sums[:, 1:2],
+                scalar2=-1.0 / E_OUT,
+                op0=ALU.add,
+                op1=ALU.mult,
+            )
+            y_copy_of[i] = y_copy
+            neg_mean_of[i] = neg_mean
+
+        def row_rstds(i):
+            squares = stage2.tile([P, E_OUT], BF16)
+            square_sum = stage2.tile([P, 1], F32)
+            nc.scalar.activation(
+                out=squares[:],
+                in_=y_copy_of[i][:],
+                func=ACT.Square,
+                bias=neg_mean_of[i][:, 0:1],
+                accum_out=square_sum[:],
+            )
+            var_eps = stage2.tile([P, 1], F32)
+            nc.gpsimd.tensor_scalar(
+                out=var_eps[:],
+                in0=square_sum[:],
+                scalar1=1.0 / E_OUT,
+                scalar2=LN_EPS,
+                op0=ALU.mult,
+                op1=ALU.add,
+            )
+            rstd = stage2.tile([P, 1], F32)
+            nc.gpsimd.tensor_tensor(out=rstd[:], in0=var_eps[:], in1=minus_half[:], op=ALU.pow)
+            rstd_of[i] = rstd
+
+        def centre(i):
+            centred = stage2.tile([P, E_OUT], F32)
+            for n_half in range(HALVES):
+                cols = slice(n_half * BANK, (n_half + 1) * BANK)
+                nc.vector.scalar_tensor_tensor(
+                    out=centred[:, cols],
+                    in0=y_of[i][n_half][:],
+                    scalar=neg_mean_of[i][:, 0:1],
+                    in1=ln_w_rows[:, cols],
+                    op0=ALU.add,
+                    op1=ALU.mult,
+                )
+            centred_of[i] = centred
+
+        ln_b_banks = []
+        for n_half in range(HALVES):
+            ln_b_bank = psum_keep.tile([P, BANK], F32, name="ln_b_bank%d" % n_half)
+            nc.tensor.matmul(
+                out=ln_b_bank[:],
+                lhsT=ident_bf16[:],
+                rhs=ln_b_rows[:, n_half * BANK : (n_half + 1) * BANK],
+                start=True,
+                stop=True,
+            )
+            ln_b_banks.append(ln_b_bank)
+
+        def scale_and_store(i):
+            result = stage2.tile([P, E_OUT], F32)
+            for n_half in range(HALVES):
+                cols = slice(n_half * BANK, (n_half + 1) * BANK)
+                nc.vector.scalar_tensor_tensor(
+                    out=result[:, cols],
+                    in0=centred_of[i][:, cols],
+                    scalar=rstd_of[i][:, 0:1],
+                    in1=ln_b_banks[n_half][:],
+                    op0=ALU.mult,
+                    op1=ALU.add,
+                )
+                nc.sync.dma_start(
+                    out=out_rows[:, i * E_OUT + n_half * BANK : i * E_OUT + (n_half + 1) * BANK],
+                    in_=result[:, cols],
+                )
+
+        for step in range(TILES + 2):
+            if step < TILES:
+                project(step)
+                row_means(step)
+            if 1 <= step <= TILES:
+                row_rstds(step - 1)
+                centre(step - 1)
+            if step >= 2:
+                scale_and_store(step - 2)

@@ -26,10 +26,12 @@ PASSES = E // (P * PACK)
 UNITS = PAIRS * PASSES
 BANK = 512
 HALVES = E_OUT // BANK
+FOLD = 128
 WO_CHUNK = 128
 WO_CHUNKS_PER_PASS = E_OUT // WO_CHUNK
 WO_CHUNKS = PASSES * WO_CHUNKS_PER_PASS
-WO_FIRST_UNIT = 2
+WO_FIRST_STEP = 2
+GATE_LOW_FIRST = 4 * D_GATE
 
 FLOPS = 2 * TOKENS * E * E_OUT + 2 * TOKENS * D_GATE * E
 
@@ -43,7 +45,7 @@ def tile_tnlattention_pb_kernel(tc, attn, gate_low, Wg2, Wo, ln_w, ln_b, out):
     with ExitStack() as stack:
         keep = stack.enter_context(tc.tile_pool(name="keep", bufs=1))
         stage1 = stack.enter_context(tc.tile_pool(name="stage1", bufs=3))
-        stage2 = stack.enter_context(tc.tile_pool(name="stage2", bufs=4))
+        stage2 = stack.enter_context(tc.tile_pool(name="stage2", bufs=6))
         psum_keep = stack.enter_context(tc.psum_pool(name="psum_keep", bufs=1))
         psum = stack.enter_context(tc.psum_pool(name="psum", bufs=6))
 
@@ -51,11 +53,17 @@ def tile_tnlattention_pb_kernel(tc, attn, gate_low, Wg2, Wo, ln_w, ln_b, out):
         gate_low_sb = keep.tile([P, TILES * D_GATE], BF16)
         attn_sb = keep.tile([P, TILES * E], BF16)
         wo_raw = keep.tile([P, PASSES, PACK, E_OUT], BF16)
+        ln_w_rows = keep.tile([P, E_OUT], BF16)
+        ln_b_rows = keep.tile([P, E_OUT], BF16)
+        first_gate_cols = slice(0, GATE_LOW_FIRST)
+        other_gate_cols = slice(GATE_LOW_FIRST, TILES * D_GATE)
+        nc.sync.dma_start(out=gate_low_sb[:, first_gate_cols], in_=gate_low_rows[:, first_gate_cols])
+        nc.sync.dma_start(out=wg2_sb[:], in_=Wg2)
         for pair in range(PAIRS):
-            gate_cols = slice(pair * 2 * D_GATE, (pair + 1) * 2 * D_GATE)
-            nc.sync.dma_start(out=gate_low_sb[:, gate_cols], in_=gate_low_rows[:, gate_cols])
-            if pair == 0:
-                nc.sync.dma_start(out=wg2_sb[:], in_=Wg2)
+            if pair == 1:
+                nc.sync.dma_start(
+                    out=gate_low_sb[:, other_gate_cols], in_=gate_low_rows[:, other_gate_cols]
+                )
             attn_cols = slice(pair * 2 * E, (pair + 1) * 2 * E)
             nc.sync.dma_start(out=attn_sb[:, attn_cols], in_=attn_rows[:, attn_cols])
             if 1 <= pair <= PASSES:
@@ -66,22 +74,22 @@ def tile_tnlattention_pb_kernel(tc, attn, gate_low, Wg2, Wo, ln_w, ln_b, out):
                         "(p t) n -> p t n", t=PACK
                     ),
                 )
-        ln_w_rows = keep.tile([P, E_OUT], BF16)
         nc.sync.dma_start(out=ln_w_rows[:], in_=ln_w.partition_broadcast(P))
-        ln_b_rows = keep.tile([P, E_OUT], BF16)
         nc.sync.dma_start(out=ln_b_rows[:], in_=ln_b.partition_broadcast(P))
 
         ident_bf16 = keep.tile([P, P], BF16)
         make_identity(nc, ident_bf16[:])
         ident_f32 = keep.tile([P, P], F32)
         make_identity(nc, ident_f32[:])
-        minus_half = keep.tile([P, 1], F32)
-        nc.gpsimd.memset(minus_half[:], -0.5)
+        zero_column = keep.tile([P, 1], F32)
+        nc.vector.memset(zero_column[:], 0.0)
+        eps_column = keep.tile([P, 1], F32)
+        nc.gpsimd.tensor_scalar(
+            out=eps_column[:], in0=zero_column[:], scalar1=0.0, scalar2=LN_EPS, op0=ALU.mult, op1=ALU.add
+        )
 
-        table_in = keep.tile([P, 1], F32)
-        nc.vector.memset(table_in[:], 0.0)
         table_out = keep.tile([P, 1], F32)
-        nc.scalar.activation(out=table_out[:], in_=table_in[:], func=ACT.Sigmoid)
+        nc.scalar.activation(out=table_out[:], in_=zero_column[:], func=ACT.Sigmoid)
 
         wg2_by_word = wg2_sb[:].rearrange("d (g p t) -> d g t p", g=PASSES, t=PACK)
         attn_words = attn_sb[:].bitcast(F32)
@@ -93,15 +101,23 @@ def tile_tnlattention_pb_kernel(tc, attn, gate_low, Wg2, Wo, ln_w, ln_b, out):
         h_scales = keep.tile([P, PAIRS, PASSES, PAIR_TOKENS], U8, align_bytes=64)
         gate_lowT = keep.tile([P, TILES * P], BF16)
 
+        sig_of = {}
+        h_grouped_of = {}
+
         def wo_chunk(chunk):
-            g, quarter = divmod(chunk, WO_CHUNKS_PER_PASS)
-            return g, slice(quarter * WO_CHUNK, (quarter + 1) * WO_CHUNK)
+            g, part = divmod(chunk, WO_CHUNKS_PER_PASS)
+            return g, slice(part * WO_CHUNK, (part + 1) * WO_CHUNK)
 
         def regroup_wo(chunk):
             g, cols = wo_chunk(chunk)
             grouped = wo_grouped[:, g, cols, :].rearrange("p (c i) t -> p c t i", i=4)
             raw = wo_raw[:, g, :, cols].rearrange("p t (c i) -> p c t i", i=4)
-            nc.scalar.copy(out=grouped, in_=raw)
+            if chunk % 2 == 1:
+                nc.gpsimd.tensor_scalar(
+                    out=grouped, in0=raw, scalar1=1.0, scalar2=0.0, op0=ALU.mult, op1=ALU.add
+                )
+            else:
+                nc.scalar.copy(out=grouped, in_=raw)
 
         def quantise_wo(chunk):
             g, cols = wo_chunk(chunk)
@@ -112,7 +128,7 @@ def tile_tnlattention_pb_kernel(tc, attn, gate_low, Wg2, Wo, ln_w, ln_b, out):
             )
 
         def turn_gate_low(pair):
-            turned = psum.tile([P, PAIR_TOKENS], BF16, tag="bank")
+            turned = psum_keep.tile([P, PAIR_TOKENS], BF16, tag="short")
             for half in range(2):
                 i = 2 * pair + half
                 nc.tensor.transpose(
@@ -120,11 +136,11 @@ def tile_tnlattention_pb_kernel(tc, attn, gate_low, Wg2, Wo, ln_w, ln_b, out):
                     in_=gate_low_sb[:, i * D_GATE : (i + 1) * D_GATE],
                     identity=ident_bf16[:],
                 )
-            nc.vector.tensor_copy(
+            nc.scalar.copy(
                 out=gate_lowT[:, pair * PAIR_TOKENS : (pair + 1) * PAIR_TOKENS], in_=turned[:]
             )
 
-        def gated_unit(pair, g, h_grouped):
+        def gate(pair, g):
             sig = stage1.tile([P, PAIR_TOKENS, PACK], F32)
             for half in range(2):
                 i = 2 * pair + half
@@ -142,6 +158,12 @@ def tile_tnlattention_pb_kernel(tc, attn, gate_low, Wg2, Wo, ln_w, ln_b, out):
                     in_=gateT[:].rearrange("p t m -> p m t"),
                     func=ACT.Sigmoid,
                 )
+            sig_of[pair, g] = sig
+
+        def apply_gate(pair, g):
+            if g == 0:
+                h_grouped = stage1.tile([P, PASSES, PAIR_TOKENS, PACK], BF16, align_bytes=64)
+                h_grouped_of[pair] = h_grouped
             attnT = psum.tile([P, BANK], F32, tag="bank")
             for u in range(2):
                 for half in range(2):
@@ -152,47 +174,57 @@ def tile_tnlattention_pb_kernel(tc, attn, gate_low, Wg2, Wo, ln_w, ln_b, out):
                         identity=ident_f32[:],
                     )
             nc.vector.tensor_tensor(
-                out=h_grouped[:, g].rearrange("p m (u e) -> p m u e", e=2),
+                out=h_grouped_of[pair][:, g].rearrange("p m (u e) -> p m u e", e=2),
                 in0=attnT[:].bitcast(BF16).rearrange("p (u m e) -> p m u e", u=2, e=2),
-                in1=sig[:].rearrange("p m (u e) -> p m u e", e=2),
+                in1=sig_of[pair, g][:].rearrange("p m (u e) -> p m u e", e=2),
                 op=ALU.mult,
             )
 
-        def quantise_h(pair, h_grouped):
+        def quantise_h(pair):
             nc.vector.quantize_mx(
                 out=h_codes[:, pair].rearrange("p g m -> p (g m)").bitcast(FP8X4),
                 scales=h_scales[:, pair].rearrange("p g m -> p (g m)"),
-                in_=h_grouped[:].rearrange("p g m t -> p (g m t)"),
+                in_=h_grouped_of[pair][:].rearrange("p g m t -> p (g m t)"),
             )
 
-        h_grouped_of = {}
-        turn_gate_low(0)
-        for step in range(UNITS + WO_FIRST_UNIT + 1):
-            pair, g = divmod(step, PASSES)
-            if step < UNITS:
-                if g == 0:
-                    h_grouped = stage1.tile([P, PASSES, PAIR_TOKENS, PACK], BF16, align_bytes=64)
-                    h_grouped_of[pair] = h_grouped
-                if g == PASSES - 1 and pair + 1 < PAIRS:
-                    turn_gate_low(pair + 1)
-                gated_unit(pair, g, h_grouped_of[pair])
-            chunk = step - WO_FIRST_UNIT
-            if 0 <= chunk < WO_CHUNKS:
-                regroup_wo(chunk)
-            if 0 <= chunk - 1 < WO_CHUNKS:
-                quantise_wo(chunk - 1)
-            if g == 0 and 1 <= pair <= PAIRS:
-                quantise_h(pair - 1, h_grouped_of[pair - 1])
-
+        folded_of = {}
         y_of = {}
         y_copy_of = {}
+        half_means_of = {}
         neg_mean_of = {}
+        square_sums_of = {}
         rstd_of = {}
         centred_of = {}
+
+        def summed_by_tensor(i):
+            return i % 2 == 0 and i > 1
+
+        def finished_by_gpsimd(i):
+            return i % 2 == 0 and i < 12
+
+        def fold_columns(i):
+            pair, half = divmod(i, 2)
+            tokens = slice(half * P, (half + 1) * P)
+            folded = psum_keep.tile([P, FOLD], F32, tag="short")
+            for g in range(PASSES):
+                for n_group in range(E_OUT // FOLD):
+                    cols = slice(n_group * FOLD, (n_group + 1) * FOLD)
+                    nc.tensor.matmul_mx(
+                        out=folded[:],
+                        lhsT=h_codes[:, pair, g, tokens].bitcast(FP8X4),
+                        lhsT_scale=h_scales[:, pair, g, tokens],
+                        rhs=wo_codes[:, g, cols].bitcast(FP8X4),
+                        rhs_scale=wo_scales[:, g, cols],
+                        start=(g == 0 and n_group == 0),
+                        stop=(g == PASSES - 1 and n_group == E_OUT // FOLD - 1),
+                    )
+            folded_of[i] = folded
 
         def project(i):
             pair, half = divmod(i, 2)
             tokens = slice(half * P, (half + 1) * P)
+            if summed_by_tensor(i):
+                fold_columns(i)
             banks = []
             for n_half in range(HALVES):
                 cols = slice(n_half * BANK, (n_half + 1) * BANK)
@@ -211,99 +243,189 @@ def tile_tnlattention_pb_kernel(tc, attn, gate_low, Wg2, Wo, ln_w, ln_b, out):
             y_of[i] = banks
 
         def row_means(i):
+            if summed_by_tensor(i):
+                neg_mean = stage2.tile([P, 1], F32)
+                folded_copy = stage2.tile([P, FOLD], BF16)
+                nc.scalar.activation(
+                    out=folded_copy[:],
+                    in_=folded_of[i][:],
+                    func=ACT.Identity,
+                    scale=-1.0 / E_OUT,
+                    accum_out=neg_mean[:],
+                )
+                neg_mean_of[i] = neg_mean
+                return
             y_copy = stage2.tile([P, E_OUT], F32)
-            sums = stage2.tile([P, HALVES], F32)
+            half_means = stage2.tile([P, HALVES], F32)
             for n_half in range(HALVES):
                 nc.scalar.activation(
                     out=y_copy[:, n_half * BANK : (n_half + 1) * BANK],
                     in_=y_of[i][n_half][:],
                     func=ACT.Identity,
-                    accum_out=sums[:, n_half : n_half + 1],
+                    scale=-1.0 / E_OUT,
+                    accum_out=half_means[:, n_half : n_half + 1],
                 )
-            neg_mean = stage2.tile([P, 1], F32)
-            nc.gpsimd.tensor_scalar(
-                out=neg_mean[:],
-                in0=sums[:, 0:1],
-                scalar1=sums[:, 1:2],
-                scalar2=-1.0 / E_OUT,
+            y_copy_of[i] = y_copy
+            half_means_of[i] = half_means
+
+        def join_means(i):
+            if not summed_by_tensor(i):
+                neg_mean = stage2.tile([P, 1], F32)
+                nc.scalar.activation(
+                    out=neg_mean[:],
+                    in_=half_means_of[i][:, 0:1],
+                    func=ACT.Identity,
+                    bias=half_means_of[i][:, 1:2],
+                )
+                neg_mean_of[i] = neg_mean
+
+        def square(i, n_half):
+            if summed_by_tensor(i):
+                if n_half == 0:
+                    square_sums_of[i] = stage2.tile([P, HALVES], F32, name="half_square_sums")
+                squares = stage2.tile([P, E_OUT], BF16)
+                nc.scalar.activation(
+                    out=squares[:, :BANK],
+                    in_=y_of[i][n_half][:],
+                    func=ACT.Square,
+                    bias=neg_mean_of[i][:, 0:1],
+                    accum_out=square_sums_of[i][:, n_half : n_half + 1],
+                )
+            elif n_half == 0:
+                square_sums_of[i] = stage2.tile([P, 1], F32, name="square_sum")
+                squares = stage2.tile([P, E_OUT], BF16)
+                nc.scalar.activation(
+                    out=squares[:],
+                    in_=y_copy_of[i][:],
+                    func=ACT.Square,
+                    scale=-1.0 * E_OUT,
+                    bias=neg_mean_of[i][:, 0:1],
+                    accum_out=square_sums_of[i][:],
+                )
+
+        def join_squares(i):
+            if summed_by_tensor(i):
+                square_sum = stage2.tile([P, 1], F32)
+                nc.scalar.activation(
+                    out=square_sum[:],
+                    in_=square_sums_of[i][:, 0:1],
+                    func=ACT.Identity,
+                    bias=square_sums_of[i][:, 1:2],
+                )
+                square_sums_of[i] = square_sum
+
+        def row_rstd(i):
+            rstd = stage2.tile([P, 1], F32)
+            nc.scalar.activation(
+                out=rstd[:],
+                in_=square_sums_of[i][:, 0:1],
+                func=ACT.Abs_reciprocal_sqrt,
+                scale=1.0 / E_OUT,
+                bias=eps_column[:, 0:1],
+            )
+            rstd_of[i] = rstd
+
+        def centre(i, n_half):
+            if n_half == 0:
+                centred_of[i] = stage2.tile([P, E_OUT], F32, name="centred")
+            cols = slice(n_half * BANK, (n_half + 1) * BANK)
+            nc.vector.scalar_tensor_tensor(
+                out=centred_of[i][:, cols],
+                in0=y_of[i][n_half][:],
+                scalar=neg_mean_of[i][:, 0:1],
+                in1=ln_w_rows[:, cols],
                 op0=ALU.add,
                 op1=ALU.mult,
             )
-            y_copy_of[i] = y_copy
-            neg_mean_of[i] = neg_mean
 
-        def row_rstds(i):
-            squares = stage2.tile([P, E_OUT], BF16)
-            square_sum = stage2.tile([P, 1], F32)
-            nc.scalar.activation(
-                out=squares[:],
-                in_=y_copy_of[i][:],
-                func=ACT.Square,
-                bias=neg_mean_of[i][:, 0:1],
-                accum_out=square_sum[:],
-            )
-            var_eps = stage2.tile([P, 1], F32)
-            nc.gpsimd.tensor_scalar(
-                out=var_eps[:],
-                in0=square_sum[:],
-                scalar1=1.0 / E_OUT,
-                scalar2=LN_EPS,
-                op0=ALU.mult,
-                op1=ALU.add,
-            )
-            rstd = stage2.tile([P, 1], F32)
-            nc.gpsimd.tensor_tensor(out=rstd[:], in0=var_eps[:], in1=minus_half[:], op=ALU.pow)
-            rstd_of[i] = rstd
+        ln_b_bank = psum_keep.tile([P, E_OUT], BF16)
 
-        def centre(i):
-            centred = stage2.tile([P, E_OUT], F32)
+        def spread_ln_b():
             for n_half in range(HALVES):
-                cols = slice(n_half * BANK, (n_half + 1) * BANK)
-                nc.vector.scalar_tensor_tensor(
-                    out=centred[:, cols],
-                    in0=y_of[i][n_half][:],
-                    scalar=neg_mean_of[i][:, 0:1],
-                    in1=ln_w_rows[:, cols],
-                    op0=ALU.add,
-                    op1=ALU.mult,
+                nc.tensor.matmul(
+                    out=ln_b_bank[:, n_half * BANK : (n_half + 1) * BANK],
+                    lhsT=ident_bf16[:],
+                    rhs=ln_b_rows[:, n_half * BANK : (n_half + 1) * BANK],
+                    start=True,
+                    stop=True,
                 )
-            centred_of[i] = centred
-
-        ln_b_banks = []
-        for n_half in range(HALVES):
-            ln_b_bank = psum_keep.tile([P, BANK], F32, name="ln_b_bank%d" % n_half)
-            nc.tensor.matmul(
-                out=ln_b_bank[:],
-                lhsT=ident_bf16[:],
-                rhs=ln_b_rows[:, n_half * BANK : (n_half + 1) * BANK],
-                start=True,
-                stop=True,
-            )
-            ln_b_banks.append(ln_b_bank)
 
         def scale_and_store(i):
-            result = stage2.tile([P, E_OUT], F32)
             for n_half in range(HALVES):
+                result = stage2.tile([P, BANK], F32)
                 cols = slice(n_half * BANK, (n_half + 1) * BANK)
-                nc.vector.scalar_tensor_tensor(
-                    out=result[:, cols],
-                    in0=centred_of[i][:, cols],
-                    scalar=rstd_of[i][:, 0:1],
-                    in1=ln_b_banks[n_half][:],
-                    op0=ALU.mult,
-                    op1=ALU.add,
-                )
+                if finished_by_gpsimd(i):
+                    scaled = stage2.tile([P, BANK], F32)
+                    nc.gpsimd.tensor_scalar(
+                        out=scaled[:],
+                        in0=centred_of[i][:, cols],
+                        scalar1=rstd_of[i][:, 0:1],
+                        scalar2=0.0,
+                        op0=ALU.mult,
+                        op1=ALU.add,
+                    )
+                    nc.gpsimd.tensor_tensor(
+                        out=result[:], in0=scaled[:], in1=ln_b_rows[:, cols], op=ALU.add
+                    )
+                else:
+                    nc.vector.scalar_tensor_tensor(
+                        out=result[:],
+                        in0=centred_of[i][:, cols],
+                        scalar=rstd_of[i][:, 0:1],
+                        in1=ln_b_bank[:, cols],
+                        op0=ALU.mult,
+                        op1=ALU.add,
+                    )
                 nc.sync.dma_start(
                     out=out_rows[:, i * E_OUT + n_half * BANK : i * E_OUT + (n_half + 1) * BANK],
-                    in_=result[:, cols],
+                    in_=result[:],
                 )
 
-        for step in range(TILES + 2):
-            if step < TILES:
-                project(step)
-                row_means(step)
-            if 1 <= step <= TILES:
-                row_rstds(step - 1)
-                centre(step - 1)
-            if step >= 2:
-                scale_and_store(step - 2)
+        with tc.manual_schedule():
+            next_turn = 0
+            next_chunk = 0
+            waiting_chunks = []
+            for step in range(UNITS + TILES + 2):
+                pair, g = divmod(step, PASSES)
+                new_chunks = []
+                if step < UNITS:
+                    while next_turn < PAIRS and next_turn <= pair + 1:
+                        turn_gate_low(next_turn)
+                        next_turn += 1
+                    gate(pair, g)
+                if step >= WO_FIRST_STEP:
+                    for count in range(2 - step % 2):
+                        if next_chunk < WO_CHUNKS:
+                            regroup_wo(next_chunk)
+                            new_chunks.append(next_chunk)
+                            next_chunk += 1
+                if step == UNITS - 1:
+                    nc.scalar.activation(
+                        out=table_out[:], in_=eps_column[:], func=ACT.Abs_reciprocal_sqrt
+                    )
+                    spread_ln_b()
+                tile_now = step - UNITS
+                if 0 <= tile_now < TILES:
+                    project(tile_now)
+                    row_means(tile_now)
+                if step < UNITS:
+                    apply_gate(pair, g)
+                for chunk in waiting_chunks:
+                    quantise_wo(chunk)
+                waiting_chunks = new_chunks
+                if g == 0 and 1 <= pair <= PAIRS:
+                    quantise_h(pair - 1)
+                if 2 <= tile_now:
+                    join_squares(tile_now - 2)
+                if 0 <= tile_now < TILES:
+                    join_means(tile_now)
+                if 1 <= tile_now <= TILES:
+                    centre(tile_now - 1, 0)
+                    square(tile_now - 1, 0)
+                if 2 <= tile_now:
+                    row_rstd(tile_now - 2)
+                if 1 <= tile_now <= TILES:
+                    centre(tile_now - 1, 1)
+                    square(tile_now - 1, 1)
+                if 2 <= tile_now:
+                    scale_and_store(tile_now - 2)

@@ -92,6 +92,9 @@ def tile_tnlattention_pb_kernel(tc, attn, gate_low, Wg2, Wo, ln_w, ln_b, out):
         nc.scalar.activation(out=table_out[:], in_=zero_column[:], func=ACT.Sigmoid)
 
         wg2_by_word = wg2_sb[:].rearrange("d (g p t) -> d g t p", g=PASSES, t=PACK)
+        wg2_sorted = keep.tile([P, PASSES, PACK, P], BF16)
+        for g in range(PASSES):
+            nc.vector.tensor_copy(out=wg2_sorted[:, g], in_=wg2_by_word[:, g])
         attn_words = attn_sb[:].bitcast(F32)
 
         wo_grouped = keep.tile([P, PASSES, E_OUT, PACK], BF16, align_bytes=64)
@@ -142,13 +145,14 @@ def tile_tnlattention_pb_kernel(tc, attn, gate_low, Wg2, Wo, ln_w, ln_b, out):
 
         def gate(pair, g):
             sig = stage1.tile([P, PAIR_TOKENS, PACK], F32)
+            weights = wg2_by_word if pair == 0 else wg2_sorted
             for half in range(2):
                 i = 2 * pair + half
                 gateT = psum.tile([P, PACK, P], F32, tag="bank")
                 for t in range(PACK):
                     nc.tensor.matmul(
                         out=gateT[:, t, :],
-                        lhsT=wg2_by_word[:, g, t, :],
+                        lhsT=weights[:, g, t, :],
                         rhs=gate_lowT[:, i * P : (i + 1) * P],
                         start=True,
                         stop=True,

@@ -47,7 +47,7 @@ def tile_tnlattention_pb_kernel(tc, attn, gate_low, Wg2, Wo, ln_w, ln_b, out):
         stage1 = stack.enter_context(tc.tile_pool(name="stage1", bufs=3))
         stage2 = stack.enter_context(tc.tile_pool(name="stage2", bufs=6))
         psum_keep = stack.enter_context(tc.psum_pool(name="psum_keep", bufs=1))
-        psum = stack.enter_context(tc.psum_pool(name="psum", bufs=6))
+        psum = stack.enter_context(tc.psum_pool(name="psum", bufs=7))
 
         wg2_sb = keep.tile([P, E], BF16)
         gate_low_sb = keep.tile([P, TILES * D_GATE], BF16)
@@ -131,7 +131,7 @@ def tile_tnlattention_pb_kernel(tc, attn, gate_low, Wg2, Wo, ln_w, ln_b, out):
             )
 
         def turn_gate_low(pair):
-            turned = psum_keep.tile([P, PAIR_TOKENS], BF16, tag="short")
+            turned = psum.tile([P, PAIR_TOKENS], BF16, tag="bank")
             for half in range(2):
                 i = 2 * pair + half
                 nc.tensor.transpose(
@@ -197,19 +197,20 @@ def tile_tnlattention_pb_kernel(tc, attn, gate_low, Wg2, Wo, ln_w, ln_b, out):
         half_means_of = {}
         neg_mean_of = {}
         square_sums_of = {}
+        share_of = {}
         rstd_of = {}
         centred_of = {}
 
         def summed_by_tensor(i):
-            return i % 2 == 0 and i > 1
+            return i % 3 != 0 and i > 1
 
         def finished_by_gpsimd(i):
-            return i % 2 == 0 and i < 12
+            return i % 2 == 0 and i < 14
 
         def fold_columns(i):
             pair, half = divmod(i, 2)
             tokens = slice(half * P, (half + 1) * P)
-            folded = psum_keep.tile([P, FOLD], F32, tag="short")
+            folded = psum.tile([P, FOLD], F32, tag="bank")
             for g in range(PASSES):
                 for n_group in range(E_OUT // FOLD):
                     cols = slice(n_group * FOLD, (n_group + 1) * FOLD)
@@ -307,25 +308,30 @@ def tile_tnlattention_pb_kernel(tc, attn, gate_low, Wg2, Wo, ln_w, ln_b, out):
                     accum_out=square_sums_of[i][:],
                 )
 
-        def join_squares(i):
+        def first_half_variance(i):
             if summed_by_tensor(i):
-                square_sum = stage2.tile([P, 1], F32)
+                share = stage2.tile([P, 1], F32)
                 nc.scalar.activation(
-                    out=square_sum[:],
+                    out=share[:],
                     in_=square_sums_of[i][:, 0:1],
                     func=ACT.Identity,
-                    bias=square_sums_of[i][:, 1:2],
+                    scale=1.0 / E_OUT,
+                    bias=eps_column[:, 0:1],
                 )
-                square_sums_of[i] = square_sum
+                share_of[i] = share
 
         def row_rstd(i):
             rstd = stage2.tile([P, 1], F32)
+            if summed_by_tensor(i):
+                last_sum, rest = square_sums_of[i][:, 1:2], share_of[i]
+            else:
+                last_sum, rest = square_sums_of[i][:, 0:1], eps_column
             nc.scalar.activation(
                 out=rstd[:],
-                in_=square_sums_of[i][:, 0:1],
+                in_=last_sum,
                 func=ACT.Abs_reciprocal_sqrt,
                 scale=1.0 / E_OUT,
-                bias=eps_column[:, 0:1],
+                bias=rest[:, 0:1],
             )
             rstd_of[i] = rstd
 
@@ -420,16 +426,15 @@ def tile_tnlattention_pb_kernel(tc, attn, gate_low, Wg2, Wo, ln_w, ln_b, out):
                 if g == 0 and 1 <= pair <= PAIRS:
                     quantise_h(pair - 1)
                 if 2 <= tile_now:
-                    join_squares(tile_now - 2)
-                if 0 <= tile_now < TILES:
-                    join_means(tile_now)
+                    row_rstd(tile_now - 2)
                 if 1 <= tile_now <= TILES:
                     centre(tile_now - 1, 0)
                     square(tile_now - 1, 0)
-                if 2 <= tile_now:
-                    row_rstd(tile_now - 2)
+                if 0 <= tile_now < TILES:
+                    join_means(tile_now)
                 if 1 <= tile_now <= TILES:
                     centre(tile_now - 1, 1)
                     square(tile_now - 1, 1)
+                    first_half_variance(tile_now - 1)
                 if 2 <= tile_now:
                     scale_and_store(tile_now - 2)

@@ -30,8 +30,9 @@ FOLD = 128
 WO_CHUNK = 128
 WO_CHUNKS_PER_PASS = E_OUT // WO_CHUNK
 WO_CHUNKS = PASSES * WO_CHUNKS_PER_PASS
-WO_FIRST_STEP = 2
+WO_FIRST_STEP = 1
 GATE_LOW_FIRST = 4 * D_GATE
+GATE_LOW_SECOND = 8 * D_GATE
 
 FLOPS = 2 * TOKENS * E * E_OUT + 2 * TOKENS * D_GATE * E
 
@@ -52,27 +53,30 @@ def tile_tnlattention_pb_kernel(tc, attn, gate_low, Wg2, Wo, ln_w, ln_b, out):
         wg2_sb = keep.tile([P, E], BF16)
         gate_low_sb = keep.tile([P, TILES * D_GATE], BF16)
         attn_sb = keep.tile([P, TILES * E], BF16)
-        wo_raw = keep.tile([P, PASSES, PACK, E_OUT], BF16)
+        wo_raw = keep.tile([P, PASSES, HALVES, PACK, BANK], BF16)
         ln_w_rows = keep.tile([P, E_OUT], BF16)
         ln_b_rows = keep.tile([P, E_OUT], BF16)
         first_gate_cols = slice(0, GATE_LOW_FIRST)
-        other_gate_cols = slice(GATE_LOW_FIRST, TILES * D_GATE)
+        second_gate_cols = slice(GATE_LOW_FIRST, GATE_LOW_SECOND)
+        other_gate_cols = slice(GATE_LOW_SECOND, TILES * D_GATE)
         nc.sync.dma_start(out=gate_low_sb[:, first_gate_cols], in_=gate_low_rows[:, first_gate_cols])
         nc.sync.dma_start(out=wg2_sb[:], in_=Wg2)
         for pair in range(PAIRS):
+            attn_cols = slice(pair * 2 * E, (pair + 1) * 2 * E)
+            nc.sync.dma_start(out=attn_sb[:, attn_cols], in_=attn_rows[:, attn_cols])
+            if pair == 0:
+                nc.sync.dma_start(
+                    out=gate_low_sb[:, second_gate_cols], in_=gate_low_rows[:, second_gate_cols]
+                )
+            if 1 <= pair <= PASSES:
+                g = pair - 1
+                wo_rows = Wo[g * P * PACK : (g + 1) * P * PACK, :].rearrange("(p t) n -> p t n", t=PACK)
+                for n_half in range(HALVES):
+                    cols = slice(n_half * BANK, (n_half + 1) * BANK)
+                    nc.sync.dma_start(out=wo_raw[:, g, n_half], in_=wo_rows[:, :, cols])
             if pair == 1:
                 nc.sync.dma_start(
                     out=gate_low_sb[:, other_gate_cols], in_=gate_low_rows[:, other_gate_cols]
-                )
-            attn_cols = slice(pair * 2 * E, (pair + 1) * 2 * E)
-            nc.sync.dma_start(out=attn_sb[:, attn_cols], in_=attn_rows[:, attn_cols])
-            if 1 <= pair <= PASSES:
-                g = pair - 1
-                nc.sync.dma_start(
-                    out=wo_raw[:, g],
-                    in_=Wo[g * P * PACK : (g + 1) * P * PACK, :].rearrange(
-                        "(p t) n -> p t n", t=PACK
-                    ),
                 )
         nc.sync.dma_start(out=ln_w_rows[:], in_=ln_w.partition_broadcast(P))
         nc.sync.dma_start(out=ln_b_rows[:], in_=ln_b.partition_broadcast(P))
@@ -111,11 +115,15 @@ def tile_tnlattention_pb_kernel(tc, attn, gate_low, Wg2, Wo, ln_w, ln_b, out):
             g, part = divmod(chunk, WO_CHUNKS_PER_PASS)
             return g, slice(part * WO_CHUNK, (part + 1) * WO_CHUNK)
 
+        def regrouped_by_gpsimd(chunk):
+            return chunk % 4 != 3
+
         def regroup_wo(chunk):
             g, cols = wo_chunk(chunk)
             grouped = wo_grouped[:, g, cols, :].rearrange("p (c i) t -> p c t i", i=4)
-            raw = wo_raw[:, g, :, cols].rearrange("p t (c i) -> p c t i", i=4)
-            if chunk % 2 == 1:
+            n_half, first = divmod(cols.start, BANK)
+            raw = wo_raw[:, g, n_half, :, first : first + WO_CHUNK].rearrange("p t (c i) -> p c t i", i=4)
+            if regrouped_by_gpsimd(chunk):
                 nc.gpsimd.tensor_scalar(
                     out=grouped, in0=raw, scalar1=1.0, scalar2=0.0, op0=ALU.mult, op1=ALU.add
                 )
@@ -202,10 +210,10 @@ def tile_tnlattention_pb_kernel(tc, attn, gate_low, Wg2, Wo, ln_w, ln_b, out):
         centred_of = {}
 
         def summed_by_tensor(i):
-            return i % 3 != 0 and i > 1
+            return i % 3 != 1
 
         def finished_by_gpsimd(i):
-            return i % 2 == 0 and i < 14
+            return i % 3 == 0 and i < 14
 
         def fold_columns(i):
             pair, half = divmod(i, 2)
@@ -403,12 +411,12 @@ def tile_tnlattention_pb_kernel(tc, attn, gate_low, Wg2, Wo, ln_w, ln_b, out):
                         turn_gate_low(next_turn)
                         next_turn += 1
                     gate(pair, g)
-                if step >= WO_FIRST_STEP:
-                    for count in range(2 - step % 2):
-                        if next_chunk < WO_CHUNKS:
-                            regroup_wo(next_chunk)
-                            new_chunks.append(next_chunk)
-                            next_chunk += 1
+                while step >= WO_FIRST_STEP and next_chunk < WO_CHUNKS:
+                    regroup_wo(next_chunk)
+                    new_chunks.append(next_chunk)
+                    next_chunk += 1
+                    if next_chunk == WO_CHUNKS or regrouped_by_gpsimd(next_chunk):
+                        break
                 if step == UNITS - 1:
                     nc.scalar.activation(
                         out=table_out[:], in_=eps_column[:], func=ACT.Abs_reciprocal_sqrt

@@ -26,7 +26,7 @@ PASSES = E // (P * PACK)
 UNITS = PAIRS * PASSES
 BANK = 512
 HALVES = E_OUT // BANK
-FOLD = 128
+FOLD = 256
 WO_CHUNK = 128
 WO_CHUNKS_PER_PASS = E_OUT // WO_CHUNK
 WO_CHUNKS = PASSES * WO_CHUNKS_PER_PASS
@@ -208,6 +208,8 @@ def tile_tnlattention_pb_kernel(tc, attn, gate_low, Wg2, Wo, ln_w, ln_b, out):
         share_of = {}
         rstd_of = {}
         centred_of = {}
+        late_stores = []
+        new_late_stores = []
 
         def summed_by_tensor(i):
             return i % 3 != 1
@@ -370,9 +372,10 @@ def tile_tnlattention_pb_kernel(tc, attn, gate_low, Wg2, Wo, ln_w, ln_b, out):
 
         def scale_and_store(i):
             for n_half in range(HALVES):
-                result = stage2.tile([P, BANK], F32)
                 cols = slice(n_half * BANK, (n_half + 1) * BANK)
+                out_cols = out_rows[:, i * E_OUT + cols.start : i * E_OUT + cols.stop]
                 if finished_by_gpsimd(i):
+                    late_result = stage2.tile([P, BANK], F32)
                     scaled = stage2.tile([P, BANK], F32)
                     nc.gpsimd.tensor_scalar(
                         out=scaled[:],
@@ -383,9 +386,11 @@ def tile_tnlattention_pb_kernel(tc, attn, gate_low, Wg2, Wo, ln_w, ln_b, out):
                         op1=ALU.add,
                     )
                     nc.gpsimd.tensor_tensor(
-                        out=result[:], in0=scaled[:], in1=ln_b_rows[:, cols], op=ALU.add
+                        out=late_result[:], in0=scaled[:], in1=ln_b_rows[:, cols], op=ALU.add
                     )
+                    new_late_stores.append((out_cols, late_result))
                 else:
+                    result = stage2.tile([P, BANK], F32)
                     nc.vector.scalar_tensor_tensor(
                         out=result[:],
                         in0=centred_of[i][:, cols],
@@ -394,10 +399,7 @@ def tile_tnlattention_pb_kernel(tc, attn, gate_low, Wg2, Wo, ln_w, ln_b, out):
                         op0=ALU.mult,
                         op1=ALU.add,
                     )
-                nc.sync.dma_start(
-                    out=out_rows[:, i * E_OUT + n_half * BANK : i * E_OUT + (n_half + 1) * BANK],
-                    in_=result[:],
-                )
+                    nc.sync.dma_start(out=out_cols, in_=result[:])
 
         with tc.manual_schedule():
             next_turn = 0
@@ -446,3 +448,7 @@ def tile_tnlattention_pb_kernel(tc, attn, gate_low, Wg2, Wo, ln_w, ln_b, out):
                     first_half_variance(tile_now - 1)
                 if 2 <= tile_now:
                     scale_and_store(tile_now - 2)
+                for out_cols, late_result in late_stores:
+                    nc.sync.dma_start(out=out_cols, in_=late_result[:])
+                late_stores = list(new_late_stores)
+                new_late_stores.clear()

@@ -130,8 +130,9 @@ def tile_tnlattention_pb_kernel(tc, attn, gate_low, Wg2, Wo, ln_w, ln_b, out):
             else:
                 nc.scalar.copy(out=grouped, in_=raw)
 
-        def quantise_wo(chunk):
-            g, cols = wo_chunk(chunk)
+        def quantise_wo(last_chunk):
+            g, cols = wo_chunk(last_chunk)
+            cols = slice(cols.start - WO_CHUNK, cols.stop)
             nc.vector.quantize_mx(
                 out=wo_codes[:, g, cols].bitcast(FP8X4),
                 scales=wo_scales[:, g, cols],
@@ -212,7 +213,7 @@ def tile_tnlattention_pb_kernel(tc, attn, gate_low, Wg2, Wo, ln_w, ln_b, out):
         new_late_stores = []
 
         def summed_by_tensor(i):
-            return i % 3 != 1
+            return i % 3 != 1 and i > 0
 
         def finished_by_gpsimd(i):
             return i % 3 == 0 and i < 14
@@ -321,12 +322,13 @@ def tile_tnlattention_pb_kernel(tc, attn, gate_low, Wg2, Wo, ln_w, ln_b, out):
         def first_half_variance(i):
             if summed_by_tensor(i):
                 share = stage2.tile([P, 1], F32)
-                nc.scalar.activation(
+                nc.vector.tensor_scalar(
                     out=share[:],
-                    in_=square_sums_of[i][:, 0:1],
-                    func=ACT.Identity,
-                    scale=1.0 / E_OUT,
-                    bias=eps_column[:, 0:1],
+                    in0=square_sums_of[i][:, 0:1],
+                    scalar1=1.0 / E_OUT,
+                    scalar2=LN_EPS,
+                    op0=ALU.mult,
+                    op1=ALU.add,
                 )
                 share_of[i] = share
 
@@ -409,7 +411,7 @@ def tile_tnlattention_pb_kernel(tc, attn, gate_low, Wg2, Wo, ln_w, ln_b, out):
                 pair, g = divmod(step, PASSES)
                 new_chunks = []
                 if step < UNITS:
-                    while next_turn < PAIRS and next_turn <= pair + 1:
+                    while next_turn < PAIRS and next_turn <= pair + 1 + g:
                         turn_gate_low(next_turn)
                         next_turn += 1
                     gate(pair, g)
@@ -431,7 +433,8 @@ def tile_tnlattention_pb_kernel(tc, attn, gate_low, Wg2, Wo, ln_w, ln_b, out):
                 if step < UNITS:
                     apply_gate(pair, g)
                 for chunk in waiting_chunks:
-                    quantise_wo(chunk)
+                    if chunk % 2 == 1:
+                        quantise_wo(chunk)
                 waiting_chunks = new_chunks
                 if g == 0 and 1 <= pair <= PAIRS:
                     quantise_h(pair - 1)
@@ -445,9 +448,10 @@ def tile_tnlattention_pb_kernel(tc, attn, gate_low, Wg2, Wo, ln_w, ln_b, out):
                 if 1 <= tile_now <= TILES:
                     centre(tile_now - 1, 1)
                     square(tile_now - 1, 1)
-                    first_half_variance(tile_now - 1)
                 if 2 <= tile_now:
                     scale_and_store(tile_now - 2)
+                if 1 <= tile_now <= TILES:
+                    first_half_variance(tile_now - 1)
                 for out_cols, late_result in late_stores:
                     nc.sync.dma_start(out=out_cols, in_=late_result[:])
                 late_stores = list(new_late_stores)

@@ -53,7 +53,8 @@ def tile_tnlattention_pb_kernel(tc, attn, gate_low, Wg2, Wo, ln_w, ln_b, out):
         wg2_sb = keep.tile([P, E], BF16)
         gate_low_sb = keep.tile([P, TILES * D_GATE], BF16)
         attn_sb = keep.tile([P, TILES * E], BF16)
-        wo_raw = keep.tile([P, PASSES, HALVES, PACK, BANK], BF16)
+        wo_first = keep.tile([P, HALVES, PACK, BANK], BF16)
+        wo_second = keep.tile([P, PACK, E_OUT], BF16)
         ln_w_rows = keep.tile([P, E_OUT], BF16)
         ln_b_rows = keep.tile([P, E_OUT], BF16)
         first_gate_cols = slice(0, GATE_LOW_FIRST)
@@ -71,9 +72,12 @@ def tile_tnlattention_pb_kernel(tc, attn, gate_low, Wg2, Wo, ln_w, ln_b, out):
             if 1 <= pair <= PASSES:
                 g = pair - 1
                 wo_rows = Wo[g * P * PACK : (g + 1) * P * PACK, :].rearrange("(p t) n -> p t n", t=PACK)
-                for n_half in range(HALVES):
-                    cols = slice(n_half * BANK, (n_half + 1) * BANK)
-                    nc.sync.dma_start(out=wo_raw[:, g, n_half], in_=wo_rows[:, :, cols])
+                if g == 0:
+                    for n_half in range(HALVES):
+                        cols = slice(n_half * BANK, (n_half + 1) * BANK)
+                        nc.sync.dma_start(out=wo_first[:, n_half], in_=wo_rows[:, :, cols])
+                else:
+                    nc.sync.dma_start(out=wo_second[:], in_=wo_rows)
             if pair == 1:
                 nc.sync.dma_start(
                     out=gate_low_sb[:, other_gate_cols], in_=gate_low_rows[:, other_gate_cols]
@@ -121,8 +125,12 @@ def tile_tnlattention_pb_kernel(tc, attn, gate_low, Wg2, Wo, ln_w, ln_b, out):
         def regroup_wo(chunk):
             g, cols = wo_chunk(chunk)
             grouped = wo_grouped[:, g, cols, :].rearrange("p (c i) t -> p c t i", i=4)
-            n_half, first = divmod(cols.start, BANK)
-            raw = wo_raw[:, g, n_half, :, first : first + WO_CHUNK].rearrange("p t (c i) -> p c t i", i=4)
+            if g == 0:
+                n_half, first = divmod(cols.start, BANK)
+                rows = wo_first[:, n_half, :, first : first + WO_CHUNK]
+            else:
+                rows = wo_second[:, :, cols]
+            raw = rows.rearrange("p t (c i) -> p c t i", i=4)
             if regrouped_by_gpsimd(chunk):
                 nc.gpsimd.tensor_scalar(
                     out=grouped, in0=raw, scalar1=1.0, scalar2=0.0, op0=ALU.mult, op1=ALU.add
@@ -425,11 +433,12 @@ def tile_tnlattention_pb_kernel(tc, attn, gate_low, Wg2, Wo, ln_w, ln_b, out):
                     nc.scalar.activation(
                         out=table_out[:], in_=eps_column[:], func=ACT.Abs_reciprocal_sqrt
                     )
-                    spread_ln_b()
                 tile_now = step - UNITS
                 if 0 <= tile_now < TILES:
                     project(tile_now)
                     row_means(tile_now)
+                if tile_now == 1:
+                    spread_ln_b()
                 if step < UNITS:
                     apply_gate(pair, g)
                 for chunk in waiting_chunks:

@@ -26,6 +26,9 @@ PASSES = E // (P * PACK)
 UNITS = PAIRS * PASSES
 BANK = 512
 HALVES = E_OUT // BANK
+WO_BEHIND_PAIRS = [1, 3]
+WARM_UP_MATMULS = 5
+WARM_UP_COLUMNS = 256
 FOLD = 256
 WO_CHUNK = 128
 WO_CHUNKS_PER_PASS = E_OUT // WO_CHUNK
@@ -69,8 +72,8 @@ def tile_tnlattention_pb_kernel(tc, attn, gate_low, Wg2, Wo, ln_w, ln_b, out):
                 nc.sync.dma_start(
                     out=gate_low_sb[:, second_gate_cols], in_=gate_low_rows[:, second_gate_cols]
                 )
-            if 1 <= pair <= PASSES:
-                g = pair - 1
+            if pair in WO_BEHIND_PAIRS:
+                g = WO_BEHIND_PAIRS.index(pair)
                 wo_rows = Wo[g * P * PACK : (g + 1) * P * PACK, :].rearrange("(p t) n -> p t n", t=PACK)
                 if g == 0:
                     for n_half in range(HALVES):
@@ -96,13 +99,30 @@ def tile_tnlattention_pb_kernel(tc, attn, gate_low, Wg2, Wo, ln_w, ln_b, out):
             out=eps_column[:], in0=zero_column[:], scalar1=0.0, scalar2=LN_EPS, op0=ALU.mult, op1=ALU.add
         )
 
+        ones = keep.tile([P, WARM_UP_COLUMNS], BF16)
+        nc.vector.memset(ones[:], 1.0)
+
+        def warm_up():
+            unread = psum.tile([P, WARM_UP_COLUMNS], F32, tag="bank")
+            for count in range(WARM_UP_MATMULS):
+                nc.tensor.matmul(
+                    out=unread[:], lhsT=ones[:, :P], rhs=ones[:], start=True, stop=True
+                )
+
         table_out = keep.tile([P, 1], F32)
         nc.scalar.activation(out=table_out[:], in_=zero_column[:], func=ACT.Sigmoid)
 
         wg2_by_word = wg2_sb[:].rearrange("d (g p t) -> d g t p", g=PASSES, t=PACK)
         wg2_sorted = keep.tile([P, PASSES, PACK, P], BF16)
         for g in range(PASSES):
-            nc.vector.tensor_copy(out=wg2_sorted[:, g], in_=wg2_by_word[:, g])
+            nc.gpsimd.tensor_scalar(
+                out=wg2_sorted[:, g],
+                in0=wg2_by_word[:, g],
+                scalar1=1.0,
+                scalar2=0.0,
+                op0=ALU.mult,
+                op1=ALU.add,
+            )
         attn_words = attn_sb[:].bitcast(F32)
 
         wo_grouped = keep.tile([P, PASSES, E_OUT, PACK], BF16, align_bytes=64)
@@ -156,9 +176,11 @@ def tile_tnlattention_pb_kernel(tc, attn, gate_low, Wg2, Wo, ln_w, ln_b, out):
                     in_=gate_low_sb[:, i * D_GATE : (i + 1) * D_GATE],
                     identity=ident_bf16[:],
                 )
-            nc.scalar.copy(
-                out=gate_lowT[:, pair * PAIR_TOKENS : (pair + 1) * PAIR_TOKENS], in_=turned[:]
-            )
+            turned_cols = gate_lowT[:, pair * PAIR_TOKENS : (pair + 1) * PAIR_TOKENS]
+            if pair < 2:
+                nc.vector.tensor_copy(out=turned_cols, in_=turned[:])
+            else:
+                nc.scalar.copy(out=turned_cols, in_=turned[:])
 
         def gate(pair, g):
             sig = stage1.tile([P, PAIR_TOKENS, PACK], F32)
@@ -412,6 +434,7 @@ def tile_tnlattention_pb_kernel(tc, attn, gate_low, Wg2, Wo, ln_w, ln_b, out):
                     nc.sync.dma_start(out=out_cols, in_=result[:])
 
         with tc.manual_schedule():
+            warm_up()
             next_turn = 0
             next_chunk = 0
             waiting_chunks = []

from contextlib import ExitStack

import concourse.mybir as mybir
from concourse.masks import make_identity

F32 = mybir.dt.float32
BF16 = mybir.dt.bfloat16
U32 = mybir.dt.uint32
U8 = mybir.dt.uint8
FP8X4 = mybir.dt.float8_e4m3fn_x4
ACT = mybir.ActivationFunctionType
ALU = mybir.AluOpType

P = 128
TOKENS = 2048
E = 1024
D_GATE = 128
E_OUT = 1024
LN_EPS = 1e-5

TILES = TOKENS // P
PAIRS = TILES // 2
PAIR_TOKENS = 2 * P
PACK = 4
PASSES = E // (P * PACK)
UNITS = PAIRS * PASSES
BANK = 512
HALVES = E_OUT // BANK
WO_BEHIND_PAIRS = [1, 3]
WARM_UP_MATMULS = 5
WARM_UP_COLUMNS = 256
FOLD = 256
WO_CHUNK = 128
WO_CHUNKS_PER_PASS = E_OUT // WO_CHUNK
WO_CHUNKS = PASSES * WO_CHUNKS_PER_PASS
WO_FIRST_STEP = 1
GATE_LOW_FIRST = 4 * D_GATE
GATE_LOW_SECOND = 8 * D_GATE

FLOPS = 2 * TOKENS * E * E_OUT + 2 * TOKENS * D_GATE * E


def tile_tnlattention_pb_kernel(tc, attn, gate_low, Wg2, Wo, ln_w, ln_b, out):
    nc = tc.nc
    attn_rows = attn.flatten_outer_dims().rearrange("(p i) e -> p (i e)", i=TILES)
    gate_low_rows = gate_low.flatten_outer_dims().rearrange("(p i) d -> p (i d)", i=TILES)
    out_rows = out.flatten_outer_dims().rearrange("(p i) n -> p (i n)", i=TILES)

    with ExitStack() as stack:
        keep = stack.enter_context(tc.tile_pool(name="keep", bufs=1))
        stage1 = stack.enter_context(tc.tile_pool(name="stage1", bufs=3))
        stage2 = stack.enter_context(tc.tile_pool(name="stage2", bufs=6))
        psum_keep = stack.enter_context(tc.psum_pool(name="psum_keep", bufs=1))
        psum = stack.enter_context(tc.psum_pool(name="psum", bufs=7))

        wg2_sb = keep.tile([P, E], BF16)
        gate_low_sb = keep.tile([P, TILES * D_GATE], BF16)
        attn_sb = keep.tile([P, TILES * E], BF16)
        wo_first = keep.tile([P, HALVES, PACK, BANK], BF16)
        wo_second = keep.tile([P, PACK, E_OUT], BF16)
        ln_w_rows = keep.tile([P, E_OUT], BF16)
        ln_b_rows = keep.tile([P, E_OUT], BF16)
        first_gate_cols = slice(0, GATE_LOW_FIRST)
        second_gate_cols = slice(GATE_LOW_FIRST, GATE_LOW_SECOND)
        other_gate_cols = slice(GATE_LOW_SECOND, TILES * D_GATE)
        nc.sync.dma_start(out=gate_low_sb[:, first_gate_cols], in_=gate_low_rows[:, first_gate_cols])
        nc.sync.dma_start(out=wg2_sb[:], in_=Wg2)
        for pair in range(PAIRS):
            attn_cols = slice(pair * 2 * E, (pair + 1) * 2 * E)
            nc.sync.dma_start(out=attn_sb[:, attn_cols], in_=attn_rows[:, attn_cols])
            if pair == 0:
                nc.sync.dma_start(
                    out=gate_low_sb[:, second_gate_cols], in_=gate_low_rows[:, second_gate_cols]
                )
            if pair in WO_BEHIND_PAIRS:
                g = WO_BEHIND_PAIRS.index(pair)
                wo_rows = Wo[g * P * PACK : (g + 1) * P * PACK, :].rearrange("(p t) n -> p t n", t=PACK)
                if g == 0:
                    for n_half in range(HALVES):
                        cols = slice(n_half * BANK, (n_half + 1) * BANK)
                        nc.sync.dma_start(out=wo_first[:, n_half], in_=wo_rows[:, :, cols])
                else:
                    nc.sync.dma_start(out=wo_second[:], in_=wo_rows)
            if pair == 1:
                nc.sync.dma_start(
                    out=gate_low_sb[:, other_gate_cols], in_=gate_low_rows[:, other_gate_cols]
                )
        nc.sync.dma_start(out=ln_w_rows[:], in_=ln_w.partition_broadcast(P))
        nc.sync.dma_start(out=ln_b_rows[:], in_=ln_b.partition_broadcast(P))

        ident_bf16 = keep.tile([P, P], BF16)
        make_identity(nc, ident_bf16[:])
        ident_f32 = keep.tile([P, P], F32)
        make_identity(nc, ident_f32[:])
        zero_column = keep.tile([P, 1], F32)
        nc.vector.memset(zero_column[:], 0.0)
        eps_column = keep.tile([P, 1], F32)
        nc.gpsimd.tensor_scalar(
            out=eps_column[:], in0=zero_column[:], scalar1=0.0, scalar2=LN_EPS, op0=ALU.mult, op1=ALU.add
        )

        ones = keep.tile([P, WARM_UP_COLUMNS], BF16)
        nc.vector.memset(ones[:], 1.0)

        def warm_up():
            unread = psum.tile([P, WARM_UP_COLUMNS], F32, tag="bank")
            for count in range(WARM_UP_MATMULS):
                nc.tensor.matmul(
                    out=unread[:], lhsT=ones[:, :P], rhs=ones[:], start=True, stop=True
                )

        table_out = keep.tile([P, 1], F32)
        nc.scalar.activation(out=table_out[:], in_=zero_column[:], func=ACT.Sigmoid)

        wg2_by_word = wg2_sb[:].rearrange("d (g p t) -> d g t p", g=PASSES, t=PACK)
        wg2_sorted = keep.tile([P, PASSES, PACK, P], BF16)
        for g in range(PASSES):
            nc.gpsimd.tensor_scalar(
                out=wg2_sorted[:, g],
                in0=wg2_by_word[:, g],
                scalar1=1.0,
                scalar2=0.0,
                op0=ALU.mult,
                op1=ALU.add,
            )
        attn_words = attn_sb[:].bitcast(F32)

        wo_grouped = keep.tile([P, PASSES, E_OUT, PACK], BF16, align_bytes=64)
        wo_codes = keep.tile([P, PASSES, E_OUT], U32, align_bytes=64)
        wo_scales = keep.tile([P, PASSES, E_OUT], U8, align_bytes=64)
        h_codes = keep.tile([P, PAIRS, PASSES, PAIR_TOKENS], U32, align_bytes=64)
        h_scales = keep.tile([P, PAIRS, PASSES, PAIR_TOKENS], U8, align_bytes=64)
        gate_lowT = keep.tile([P, TILES * P], BF16)

        sig_of = {}
        h_grouped_of = {}

        def wo_chunk(chunk):
            g, part = divmod(chunk, WO_CHUNKS_PER_PASS)
            return g, slice(part * WO_CHUNK, (part + 1) * WO_CHUNK)

        def regrouped_by_gpsimd(chunk):
            return chunk % 4 != 3

        def regroup_wo(chunk):
            g, cols = wo_chunk(chunk)
            grouped = wo_grouped[:, g, cols, :].rearrange("p (c i) t -> p c t i", i=4)
            if g == 0:
                n_half, first = divmod(cols.start, BANK)
                rows = wo_first[:, n_half, :, first : first + WO_CHUNK]
            else:
                rows = wo_second[:, :, cols]
            raw = rows.rearrange("p t (c i) -> p c t i", i=4)
            if regrouped_by_gpsimd(chunk):
                nc.gpsimd.tensor_scalar(
                    out=grouped, in0=raw, scalar1=1.0, scalar2=0.0, op0=ALU.mult, op1=ALU.add
                )
            else:
                nc.scalar.copy(out=grouped, in_=raw)

        def quantise_wo(last_chunk):
            g, cols = wo_chunk(last_chunk)
            cols = slice(cols.start - WO_CHUNK, cols.stop)
            nc.vector.quantize_mx(
                out=wo_codes[:, g, cols].bitcast(FP8X4),
                scales=wo_scales[:, g, cols],
                in_=wo_grouped[:, g, cols, :].rearrange("p n t -> p (n t)"),
            )

        def turn_gate_low(pair):
            turned = psum.tile([P, PAIR_TOKENS], BF16, tag="bank")
            for half in range(2):
                i = 2 * pair + half
                nc.tensor.transpose(
                    out=turned[:, half * P : (half + 1) * P],
                    in_=gate_low_sb[:, i * D_GATE : (i + 1) * D_GATE],
                    identity=ident_bf16[:],
                )
            turned_cols = gate_lowT[:, pair * PAIR_TOKENS : (pair + 1) * PAIR_TOKENS]
            if pair < 2:
                nc.vector.tensor_copy(out=turned_cols, in_=turned[:])
            else:
                nc.scalar.copy(out=turned_cols, in_=turned[:])

        def gate(pair, g):
            sig = stage1.tile([P, PAIR_TOKENS, PACK], F32)
            weights = wg2_by_word if pair == 0 else wg2_sorted
            for half in range(2):
                i = 2 * pair + half
                gateT = psum.tile([P, PACK, P], F32, tag="bank")
                for t in range(PACK):
                    nc.tensor.matmul(
                        out=gateT[:, t, :],
                        lhsT=weights[:, g, t, :],
                        rhs=gate_lowT[:, i * P : (i + 1) * P],
                        start=True,
                        stop=True,
                    )
                nc.scalar.activation(
                    out=sig[:, half * P : (half + 1) * P, :],
                    in_=gateT[:].rearrange("p t m -> p m t"),
                    func=ACT.Sigmoid,
                )
            sig_of[pair, g] = sig

        def apply_gate(pair, g):
            if g == 0:
                h_grouped = stage1.tile([P, PASSES, PAIR_TOKENS, PACK], BF16, align_bytes=64)
                h_grouped_of[pair] = h_grouped
            attnT = psum.tile([P, BANK], F32, tag="bank")
            for u in range(2):
                for half in range(2):
                    word0 = (2 * pair + half) * (E // 2) + 2 * g * P + u
                    nc.tensor.transpose(
                        out=attnT[:, (2 * u + half) * P : (2 * u + half + 1) * P],
                        in_=attn_words[:, word0 : word0 + 2 * P - 1 : 2],
                        identity=ident_f32[:],
                    )
            nc.vector.tensor_tensor(
                out=h_grouped_of[pair][:, g].rearrange("p m (u e) -> p m u e", e=2),
                in0=attnT[:].bitcast(BF16).rearrange("p (u m e) -> p m u e", u=2, e=2),
                in1=sig_of[pair, g][:].rearrange("p m (u e) -> p m u e", e=2),
                op=ALU.mult,
            )

        def quantise_h(pair):
            nc.vector.quantize_mx(
                out=h_codes[:, pair].rearrange("p g m -> p (g m)").bitcast(FP8X4),
                scales=h_scales[:, pair].rearrange("p g m -> p (g m)"),
                in_=h_grouped_of[pair][:].rearrange("p g m t -> p (g m t)"),
            )

        folded_of = {}
        y_of = {}
        y_copy_of = {}
        half_means_of = {}
        neg_mean_of = {}
        square_sums_of = {}
        share_of = {}
        rstd_of = {}
        centred_of = {}
        late_stores = []
        new_late_stores = []

        def summed_by_tensor(i):
            return i % 3 != 1 and i > 0

        def finished_by_gpsimd(i):
            return i % 3 == 0 and i < 14

        def fold_columns(i):
            pair, half = divmod(i, 2)
            tokens = slice(half * P, (half + 1) * P)
            folded = psum.tile([P, FOLD], F32, tag="bank")
            for g in range(PASSES):
                for n_group in range(E_OUT // FOLD):
                    cols = slice(n_group * FOLD, (n_group + 1) * FOLD)
                    nc.tensor.matmul_mx(
                        out=folded[:],
                        lhsT=h_codes[:, pair, g, tokens].bitcast(FP8X4),
                        lhsT_scale=h_scales[:, pair, g, tokens],
                        rhs=wo_codes[:, g, cols].bitcast(FP8X4),
                        rhs_scale=wo_scales[:, g, cols],
                        start=(g == 0 and n_group == 0),
                        stop=(g == PASSES - 1 and n_group == E_OUT // FOLD - 1),
                    )
            folded_of[i] = folded

        def project(i):
            pair, half = divmod(i, 2)
            tokens = slice(half * P, (half + 1) * P)
            if summed_by_tensor(i):
                fold_columns(i)
            banks = []
            for n_half in range(HALVES):
                cols = slice(n_half * BANK, (n_half + 1) * BANK)
                y = psum.tile([P, BANK], F32, tag="bank")
                for g in range(PASSES):
                    nc.tensor.matmul_mx(
                        out=y[:],
                        lhsT=h_codes[:, pair, g, tokens].bitcast(FP8X4),
                        lhsT_scale=h_scales[:, pair, g, tokens],
                        rhs=wo_codes[:, g, cols].bitcast(FP8X4),
                        rhs_scale=wo_scales[:, g, cols],
                        start=(g == 0),
                        stop=(g == PASSES - 1),
                    )
                banks.append(y)
            y_of[i] = banks

        def row_means(i):
            if summed_by_tensor(i):
                neg_mean = stage2.tile([P, 1], F32)
                folded_copy = stage2.tile([P, FOLD], BF16)
                nc.scalar.activation(
                    out=folded_copy[:],
                    in_=folded_of[i][:],
                    func=ACT.Identity,
                    scale=-1.0 / E_OUT,
                    accum_out=neg_mean[:],
                )
                neg_mean_of[i] = neg_mean
                return
            y_copy = stage2.tile([P, E_OUT], F32)
            half_means = stage2.tile([P, HALVES], F32)
            for n_half in range(HALVES):
                nc.scalar.activation(
                    out=y_copy[:, n_half * BANK : (n_half + 1) * BANK],
                    in_=y_of[i][n_half][:],
                    func=ACT.Identity,
                    scale=-1.0 / E_OUT,
                    accum_out=half_means[:, n_half : n_half + 1],
                )
            y_copy_of[i] = y_copy
            half_means_of[i] = half_means

        def join_means(i):
            if not summed_by_tensor(i):
                neg_mean = stage2.tile([P, 1], F32)
                nc.scalar.activation(
                    out=neg_mean[:],
                    in_=half_means_of[i][:, 0:1],
                    func=ACT.Identity,
                    bias=half_means_of[i][:, 1:2],
                )
                neg_mean_of[i] = neg_mean

        def square(i, n_half):
            if summed_by_tensor(i):
                if n_half == 0:
                    square_sums_of[i] = stage2.tile([P, HALVES], F32, name="half_square_sums")
                squares = stage2.tile([P, E_OUT], BF16)
                nc.scalar.activation(
                    out=squares[:, :BANK],
                    in_=y_of[i][n_half][:],
                    func=ACT.Square,
                    bias=neg_mean_of[i][:, 0:1],
                    accum_out=square_sums_of[i][:, n_half : n_half + 1],
                )
            elif n_half == 0:
                square_sums_of[i] = stage2.tile([P, 1], F32, name="square_sum")
                squares = stage2.tile([P, E_OUT], BF16)
                nc.scalar.activation(
                    out=squares[:],
                    in_=y_copy_of[i][:],
                    func=ACT.Square,
                    scale=-1.0 * E_OUT,
                    bias=neg_mean_of[i][:, 0:1],
                    accum_out=square_sums_of[i][:],
                )

        def first_half_variance(i):
            if summed_by_tensor(i):
                share = stage2.tile([P, 1], F32)
                nc.vector.tensor_scalar(
                    out=share[:],
                    in0=square_sums_of[i][:, 0:1],
                    scalar1=1.0 / E_OUT,
                    scalar2=LN_EPS,
                    op0=ALU.mult,
                    op1=ALU.add,
                )
                share_of[i] = share

        def row_rstd(i):
            rstd = stage2.tile([P, 1], F32)
            if summed_by_tensor(i):
                last_sum, rest = square_sums_of[i][:, 1:2], share_of[i]
            else:
                last_sum, rest = square_sums_of[i][:, 0:1], eps_column
            nc.scalar.activation(
                out=rstd[:],
                in_=last_sum,
                func=ACT.Abs_reciprocal_sqrt,
                scale=1.0 / E_OUT,
                bias=rest[:, 0:1],
            )
            rstd_of[i] = rstd

        def centre(i, n_half):
            if n_half == 0:
                centred_of[i] = stage2.tile([P, E_OUT], F32, name="centred")
            cols = slice(n_half * BANK, (n_half + 1) * BANK)
            nc.vector.scalar_tensor_tensor(
                out=centred_of[i][:, cols],
                in0=y_of[i][n_half][:],
                scalar=neg_mean_of[i][:, 0:1],
                in1=ln_w_rows[:, cols],
                op0=ALU.add,
                op1=ALU.mult,
            )

        ln_b_bank = psum_keep.tile([P, E_OUT], BF16)

        def spread_ln_b():
            for n_half in range(HALVES):
                nc.tensor.matmul(
                    out=ln_b_bank[:, n_half * BANK : (n_half + 1) * BANK],
                    lhsT=ident_bf16[:],
                    rhs=ln_b_rows[:, n_half * BANK : (n_half + 1) * BANK],
                    start=True,
                    stop=True,
                )

        def scale_and_store(i):
            for n_half in range(HALVES):
                cols = slice(n_half * BANK, (n_half + 1) * BANK)
                out_cols = out_rows[:, i * E_OUT + cols.start : i * E_OUT + cols.stop]
                if finished_by_gpsimd(i):
                    late_result = stage2.tile([P, BANK], F32)
                    scaled = stage2.tile([P, BANK], F32)
                    nc.gpsimd.tensor_scalar(
                        out=scaled[:],
                        in0=centred_of[i][:, cols],
                        scalar1=rstd_of[i][:, 0:1],
                        scalar2=0.0,
                        op0=ALU.mult,
                        op1=ALU.add,
                    )
                    nc.gpsimd.tensor_tensor(
                        out=late_result[:], in0=scaled[:], in1=ln_b_rows[:, cols], op=ALU.add
                    )
                    new_late_stores.append((out_cols, late_result))
                else:
                    result = stage2.tile([P, BANK], F32)
                    nc.vector.scalar_tensor_tensor(
                        out=result[:],
                        in0=centred_of[i][:, cols],
                        scalar=rstd_of[i][:, 0:1],
                        in1=ln_b_bank[:, cols],
                        op0=ALU.mult,
                        op1=ALU.add,
                    )
                    nc.sync.dma_start(out=out_cols, in_=result[:])

        with tc.manual_schedule():
            warm_up()
            next_turn = 0
            next_chunk = 0
            waiting_chunks = []
            for step in range(UNITS + TILES + 2):
                pair, g = divmod(step, PASSES)
                new_chunks = []
                if step < UNITS:
                    while next_turn < PAIRS and next_turn <= pair + 1 + g:
                        turn_gate_low(next_turn)
                        next_turn += 1
                    gate(pair, g)
                while step >= WO_FIRST_STEP and next_chunk < WO_CHUNKS:
                    regroup_wo(next_chunk)
                    new_chunks.append(next_chunk)
                    next_chunk += 1
                    if next_chunk == WO_CHUNKS or regrouped_by_gpsimd(next_chunk):
                        break
                if step == UNITS - 1:
                    nc.scalar.activation(
                        out=table_out[:], in_=eps_column[:], func=ACT.Abs_reciprocal_sqrt
                    )
                tile_now = step - UNITS
                if 0 <= tile_now < TILES:
                    project(tile_now)
                    row_means(tile_now)
                if tile_now == 1:
                    spread_ln_b()
                if step < UNITS:
                    apply_gate(pair, g)
                for chunk in waiting_chunks:
                    if chunk % 2 == 1:
                        quantise_wo(chunk)
                waiting_chunks = new_chunks
                if g == 0 and 1 <= pair <= PAIRS:
                    quantise_h(pair - 1)
                if 2 <= tile_now:
                    row_rstd(tile_now - 2)
                if 1 <= tile_now <= TILES:
                    centre(tile_now - 1, 0)
                    square(tile_now - 1, 0)
                if 0 <= tile_now < TILES:
                    join_means(tile_now)
                if 1 <= tile_now <= TILES:
                    centre(tile_now - 1, 1)
                    square(tile_now - 1, 1)
                if 2 <= tile_now:
                    scale_and_store(tile_now - 2)
                if 1 <= tile_now <= TILES:
                    first_half_variance(tile_now - 1)
                for out_cols, late_result in late_stores:
                    nc.sync.dma_start(out=out_cols, in_=late_result[:])
                late_stores = list(new_late_stores)
                new_late_stores.clear()
